import numpy as np
import ml_dtypes

BF16 = ml_dtypes.bfloat16


def bf(x):
    return np.asarray(x, np.float32).astype(BF16)


def f32(x):
    return np.asarray(x, np.float32)


def f64(x):
    return np.asarray(x).astype(np.float64)


def striped(idx):
    return np.tile(idx.reshape(-1, 16).T, (8, 1))


C, S, B, T, A, R, N = 1024, 512, 32, 4, 7, 224, 896


def setup_inputs():
    return {"emb": f32(np.random.standard_normal((C, S))), "offs": striped(np.random.permutation(np.tile(np.arange(S), 2))[:N])}


def reference(emb, offs):
    idx = offs[:16].T.reshape(-1)
    pooled = f64(emb)[:, idx].reshape(C, T, R).sum(axis=1) * (1.0 / T)
    qv = pooled[:, :B]
    attr = pooled[:, B:].reshape(C, -1, B)
    return (attr * qv[:, None, :]).reshape(C, -1)

@@ -1,0 +1,49 @@
+import concourse.mybir as mybir
+
+F32 = mybir.dt.float32
+U16 = mybir.dt.uint16
+ADD = mybir.AluOpType.add
+MULT = mybir.AluOpType.mult
+
+P = 128
+FEATURES = 1024
+WORDS = 512
+TEXTS = 224
+WORDS_PER_TEXT = 4
+SAMPLES = 32
+ATTRS = 6
+BLOCKS = FEATURES // P
+PIECE_COLS = TEXTS // 16
+
+
+def tile_feelmodel_kernel(tc, emb, offs, out):
+    nc = tc.nc
+    with (
+        tc.tile_pool(name="held", bufs=1) as held,
+        tc.tile_pool(name="tables", bufs=BLOCKS) as tables,
+        tc.tile_pool(name="work", bufs=4) as work,
+    ):
+        offsets = held.tile([P, WORDS_PER_TEXT * PIECE_COLS], U16, name="offsets")
+        nc.sync.dma_start(offsets[:], offs)
+        zero = held.tile([P, TEXTS], F32, name="zero")
+        nc.vector.memset(zero[:], 0.0)
+
+        for k in range(BLOCKS):
+            rows = slice(k * P, (k + 1) * P)
+            table = tables.tile([P, WORDS], F32, name="table")
+            nc.scalar.dma_start(table[:], emb[rows, :])
+
+            sums = zero
+            for t in range(WORDS_PER_TEXT):
+                piece = offsets[:, t * PIECE_COLS : (t + 1) * PIECE_COLS]
+                so_far = sums
+                sums = work.tile([P, TEXTS], F32, name="sums")
+                nc.vector.tensor_tensor(sums[:], table[:].indirect(piece), so_far[:], ADD)
+
+            query = sums[:, 0:SAMPLES].unsqueeze(1).to_broadcast([P, ATTRS, SAMPLES])
+            attrs = sums[:, SAMPLES:TEXTS].rearrange("p (a b) -> p a b", b=SAMPLES)
+            products = work.tile([P, ATTRS, SAMPLES], F32, name="products")
+            nc.vector.scalar_tensor_tensor(
+                products[:], attrs, 1.0 / (WORDS_PER_TEXT * WORDS_PER_TEXT), query, MULT, MULT
+            )
+            nc.sync.dma_start(out[rows, :], products[:].rearrange("p a b -> p (a b)"))

@@ -13,6 +13,7 @@ WORDS_PER_TEXT = 4
 SAMPLES = 32
 ATTRS = 6
 BLOCKS = FEATURES // P
+TOGETHER = 2
 PIECE_COLS = TEXTS // 16
 
 
@@ -21,29 +22,35 @@ def tile_feelmodel_kernel(tc, emb, offs, out):
     with (
         tc.tile_pool(name="held", bufs=1) as held,
         tc.tile_pool(name="tables", bufs=BLOCKS) as tables,
-        tc.tile_pool(name="work", bufs=4) as work,
+        tc.tile_pool(name="work", bufs=6) as work,
     ):
         offsets = held.tile([P, WORDS_PER_TEXT * PIECE_COLS], U16, name="offsets")
         nc.sync.dma_start(offsets[:], offs)
         zero = held.tile([P, TEXTS], F32, name="zero")
         nc.vector.memset(zero[:], 0.0)
 
+        tables_of = []
         for k in range(BLOCKS):
-            rows = slice(k * P, (k + 1) * P)
             table = tables.tile([P, WORDS], F32, name="table")
-            nc.scalar.dma_start(table[:], emb[rows, :])
+            nc.scalar.dma_start(table[:], emb[k * P : (k + 1) * P, :])
+            tables_of.append(table)
 
-            sums = zero
+        for first in range(0, BLOCKS, TOGETHER):
+            group = range(first, first + TOGETHER)
+
+            sums_of = {k: zero for k in group}
             for t in range(WORDS_PER_TEXT):
                 piece = offsets[:, t * PIECE_COLS : (t + 1) * PIECE_COLS]
-                so_far = sums
-                sums = work.tile([P, TEXTS], F32, name="sums")
-                nc.vector.tensor_tensor(sums[:], table[:].indirect(piece), so_far[:], ADD)
+                for k in group:
+                    sums = work.tile([P, TEXTS], F32, name="sums")
+                    nc.vector.tensor_tensor(sums[:], tables_of[k][:].indirect(piece), sums_of[k][:], ADD)
+                    sums_of[k] = sums
 
-            query = sums[:, 0:SAMPLES].unsqueeze(1).to_broadcast([P, ATTRS, SAMPLES])
-            attrs = sums[:, SAMPLES:TEXTS].rearrange("p (a b) -> p a b", b=SAMPLES)
-            products = work.tile([P, ATTRS, SAMPLES], F32, name="products")
-            nc.vector.scalar_tensor_tensor(
-                products[:], attrs, 1.0 / (WORDS_PER_TEXT * WORDS_PER_TEXT), query, MULT, MULT
-            )
-            nc.sync.dma_start(out[rows, :], products[:].rearrange("p a b -> p (a b)"))
+            for k in group:
+                query = sums_of[k][:, 0:SAMPLES].unsqueeze(1).to_broadcast([P, ATTRS, SAMPLES])
+                attrs = sums_of[k][:, SAMPLES:TEXTS].rearrange("p (a b) -> p a b", b=SAMPLES)
+                products = work.tile([P, ATTRS, SAMPLES], F32, name="products")
+                nc.vector.scalar_tensor_tensor(
+                    products[:], attrs, 1.0 / (WORDS_PER_TEXT * WORDS_PER_TEXT), query, MULT, MULT
+                )
+                nc.sync.dma_start(out[k * P : (k + 1) * P, :], products[:].rearrange("p a b -> p (a b)"))

@@ -13,7 +13,7 @@ WORDS_PER_TEXT = 4
 SAMPLES = 32
 ATTRS = 6
 BLOCKS = FEATURES // P
-TOGETHER = 2
+TOGETHER = 4
 PIECE_COLS = TEXTS // 16
 
 
@@ -22,7 +22,7 @@ def tile_feelmodel_kernel(tc, emb, offs, out):
     with (
         tc.tile_pool(name="held", bufs=1) as held,
         tc.tile_pool(name="tables", bufs=BLOCKS) as tables,
-        tc.tile_pool(name="work", bufs=6) as work,
+        tc.tile_pool(name="work", bufs=3 * TOGETHER) as work,
     ):
         offsets = held.tile([P, WORDS_PER_TEXT * PIECE_COLS], U16, name="offsets")
         nc.sync.dma_start(offsets[:], offs)

@@ -1,4 +1,5 @@
 import concourse.mybir as mybir
+from concourse.masks import make_identity
 
 F32 = mybir.dt.float32
 U16 = mybir.dt.uint16
@@ -13,8 +14,9 @@ WORDS_PER_TEXT = 4
 SAMPLES = 32
 ATTRS = 6
 BLOCKS = FEATURES // P
-TOGETHER = 4
-PIECE_COLS = TEXTS // 16
+HALF = 2 * TEXTS
+HALF_COLS = HALF // 16
+LAG = 2
 
 
 def tile_feelmodel_kernel(tc, emb, offs, out):
@@ -22,12 +24,15 @@ def tile_feelmodel_kernel(tc, emb, offs, out):
     with (
         tc.tile_pool(name="held", bufs=1) as held,
         tc.tile_pool(name="tables", bufs=BLOCKS) as tables,
-        tc.tile_pool(name="work", bufs=3 * TOGETHER) as work,
+        tc.tile_pool(name="work", bufs=BLOCKS) as work,
+        tc.psum_pool(name="psum", bufs=4) as psum,
     ):
-        offsets = held.tile([P, WORDS_PER_TEXT * PIECE_COLS], U16, name="offsets")
+        offsets = held.tile([P, 2 * HALF_COLS], U16, name="offsets")
         nc.sync.dma_start(offsets[:], offs)
-        zero = held.tile([P, TEXTS], F32, name="zero")
+        zero = held.tile([P, HALF], F32, name="zero")
         nc.vector.memset(zero[:], 0.0)
+        identity = held.tile([P, P], F32, name="identity")
+        make_identity(nc, identity[:])
 
         tables_of = []
         for k in range(BLOCKS):
@@ -35,22 +40,42 @@ def tile_feelmodel_kernel(tc, emb, offs, out):
             nc.scalar.dma_start(table[:], emb[k * P : (k + 1) * P, :])
             tables_of.append(table)
 
-        for first in range(0, BLOCKS, TOGETHER):
-            group = range(first, first + TOGETHER)
+        early_of = {}
+        sums_of = {}
 
-            sums_of = {k: zero for k in group}
-            for t in range(WORDS_PER_TEXT):
-                piece = offsets[:, t * PIECE_COLS : (t + 1) * PIECE_COLS]
-                for k in group:
-                    sums = work.tile([P, TEXTS], F32, name="sums")
-                    nc.vector.tensor_tensor(sums[:], tables_of[k][:].indirect(piece), sums_of[k][:], ADD)
-                    sums_of[k] = sums
+        def look_up_words_01(k):
+            early = work.tile([P, HALF], F32, name="early")
+            nc.vector.tensor_tensor(early[:], tables_of[k][:].indirect(offsets[:, 0:HALF_COLS]), zero[:], ADD)
+            early_of[k] = early
 
-            for k in group:
-                query = sums_of[k][:, 0:SAMPLES].unsqueeze(1).to_broadcast([P, ATTRS, SAMPLES])
-                attrs = sums_of[k][:, SAMPLES:TEXTS].rearrange("p (a b) -> p a b", b=SAMPLES)
-                products = work.tile([P, ATTRS, SAMPLES], F32, name="products")
-                nc.vector.scalar_tensor_tensor(
-                    products[:], attrs, 1.0 / (WORDS_PER_TEXT * WORDS_PER_TEXT), query, MULT, MULT
-                )
-                nc.sync.dma_start(out[k * P : (k + 1) * P, :], products[:].rearrange("p a b -> p (a b)"))
+        def look_up_words_23(k):
+            late = work.tile([P, HALF], F32, name="late")
+            nc.vector.tensor_tensor(
+                late[:], tables_of[k][:].indirect(offsets[:, HALF_COLS : 2 * HALF_COLS]), early_of[k][:], ADD
+            )
+            sums = work.tile([P, TEXTS], F32, name="sums")
+            if k < BLOCKS - 1:
+                folded = psum.tile([P, TEXTS], F32, name="folded")
+                nc.tensor.matmul(folded[:], identity[:], late[:, 0:TEXTS], start=True, stop=False)
+                nc.tensor.matmul(folded[:], identity[:], late[:, TEXTS:HALF], start=False, stop=True)
+                nc.scalar.copy(sums[:], folded[:])
+            else:
+                nc.vector.tensor_tensor(sums[:], late[:, 0:TEXTS], late[:, TEXTS:HALF], ADD)
+            sums_of[k] = sums
+
+        def multiply_and_store(k):
+            query = sums_of[k][:, 0:SAMPLES].unsqueeze(1).to_broadcast([P, ATTRS, SAMPLES])
+            attrs = sums_of[k][:, SAMPLES:TEXTS].rearrange("p (a b) -> p a b", b=SAMPLES)
+            products = work.tile([P, ATTRS, SAMPLES], F32, name="products")
+            nc.vector.scalar_tensor_tensor(
+                products[:], attrs, 1.0 / (WORDS_PER_TEXT * WORDS_PER_TEXT), query, MULT, MULT
+            )
+            nc.sync.dma_start(out[k * P : (k + 1) * P, :], products[:].rearrange("p a b -> p (a b)"))
+
+        for step in range(BLOCKS + 1 + LAG):
+            if step < BLOCKS:
+                look_up_words_01(step)
+            if 0 <= step - 1 < BLOCKS:
+                look_up_words_23(step - 1)
+            if 0 <= step - 1 - LAG:
+                multiply_and_store(step - 1 - LAG)

@@ -16,15 +16,13 @@ ATTRS = 6
 BLOCKS = FEATURES // P
 HALF = 2 * TEXTS
 HALF_COLS = HALF // 16
-LAG = 2
 
 
 def tile_feelmodel_kernel(tc, emb, offs, out):
     nc = tc.nc
     with (
         tc.tile_pool(name="held", bufs=1) as held,
-        tc.tile_pool(name="tables", bufs=BLOCKS) as tables,
-        tc.tile_pool(name="work", bufs=BLOCKS) as work,
+        tc.tile_pool(name="blocks", bufs=BLOCKS) as blocks,
         tc.psum_pool(name="psum", bufs=4) as psum,
     ):
         offsets = held.tile([P, 2 * HALF_COLS], U16, name="offsets")
@@ -36,24 +34,19 @@ def tile_feelmodel_kernel(tc, emb, offs, out):
 
         tables_of = []
         for k in range(BLOCKS):
-            table = tables.tile([P, WORDS], F32, name="table")
+            table = blocks.tile([P, WORDS], F32, name="table")
             nc.scalar.dma_start(table[:], emb[k * P : (k + 1) * P, :])
             tables_of.append(table)
 
-        early_of = {}
-        sums_of = {}
-
-        def look_up_words_01(k):
-            early = work.tile([P, HALF], F32, name="early")
+        for k in range(BLOCKS):
+            early = blocks.tile([P, HALF], F32, name="early")
             nc.vector.tensor_tensor(early[:], tables_of[k][:].indirect(offsets[:, 0:HALF_COLS]), zero[:], ADD)
-            early_of[k] = early
-
-        def look_up_words_23(k):
-            late = work.tile([P, HALF], F32, name="late")
+            late = blocks.tile([P, HALF], F32, name="late")
             nc.vector.tensor_tensor(
-                late[:], tables_of[k][:].indirect(offsets[:, HALF_COLS : 2 * HALF_COLS]), early_of[k][:], ADD
+                late[:], tables_of[k][:].indirect(offsets[:, HALF_COLS : 2 * HALF_COLS]), early[:], ADD
             )
-            sums = work.tile([P, TEXTS], F32, name="sums")
+
+            sums = blocks.tile([P, TEXTS], F32, name="sums")
             if k < BLOCKS - 1:
                 folded = psum.tile([P, TEXTS], F32, name="folded")
                 nc.tensor.matmul(folded[:], identity[:], late[:, 0:TEXTS], start=True, stop=False)
@@ -61,21 +54,11 @@ def tile_feelmodel_kernel(tc, emb, offs, out):
                 nc.scalar.copy(sums[:], folded[:])
             else:
                 nc.vector.tensor_tensor(sums[:], late[:, 0:TEXTS], late[:, TEXTS:HALF], ADD)
-            sums_of[k] = sums
 
-        def multiply_and_store(k):
-            query = sums_of[k][:, 0:SAMPLES].unsqueeze(1).to_broadcast([P, ATTRS, SAMPLES])
-            attrs = sums_of[k][:, SAMPLES:TEXTS].rearrange("p (a b) -> p a b", b=SAMPLES)
-            products = work.tile([P, ATTRS, SAMPLES], F32, name="products")
+            query = sums[:, 0:SAMPLES].unsqueeze(1).to_broadcast([P, ATTRS, SAMPLES])
+            attrs = sums[:, SAMPLES:TEXTS].rearrange("p (a b) -> p a b", b=SAMPLES)
+            products = blocks.tile([P, ATTRS, SAMPLES], F32, name="products")
             nc.vector.scalar_tensor_tensor(
                 products[:], attrs, 1.0 / (WORDS_PER_TEXT * WORDS_PER_TEXT), query, MULT, MULT
             )
             nc.sync.dma_start(out[k * P : (k + 1) * P, :], products[:].rearrange("p a b -> p (a b)"))
-
-        for step in range(BLOCKS + 1 + LAG):
-            if step < BLOCKS:
-                look_up_words_01(step)
-            if 0 <= step - 1 < BLOCKS:
-                look_up_words_23(step - 1)
-            if 0 <= step - 1 - LAG:
-                multiply_and_store(step - 1 - LAG)

@@ -5,6 +5,7 @@ F32 = mybir.dt.float32
 U16 = mybir.dt.uint16
 ADD = mybir.AluOpType.add
 MULT = mybir.AluOpType.mult
+COPY = mybir.ActivationFunctionType.Copy
 
 P = 128
 FEATURES = 1024
@@ -14,6 +15,7 @@ WORDS_PER_TEXT = 4
 SAMPLES = 32
 ATTRS = 6
 BLOCKS = FEATURES // P
+SCALAR_BLOCKS = BLOCKS - 2
 HALF = 2 * TEXTS
 HALF_COLS = HALF // 16
 
@@ -23,7 +25,8 @@ def tile_feelmodel_kernel(tc, emb, offs, out):
     with (
         tc.tile_pool(name="held", bufs=1) as held,
         tc.tile_pool(name="blocks", bufs=BLOCKS) as blocks,
-        tc.psum_pool(name="psum", bufs=4) as psum,
+        tc.tile_pool(name="one", bufs=1) as one,
+        tc.psum_pool(name="psum", bufs=2) as psum,
     ):
         offsets = held.tile([P, 2 * HALF_COLS], U16, name="offsets")
         nc.sync.dma_start(offsets[:], offs)
@@ -38,27 +41,38 @@ def tile_feelmodel_kernel(tc, emb, offs, out):
             nc.scalar.dma_start(table[:], emb[k * P : (k + 1) * P, :])
             tables_of.append(table)
 
-        for k in range(BLOCKS):
-            early = blocks.tile([P, HALF], F32, name="early")
-            nc.vector.tensor_tensor(early[:], tables_of[k][:].indirect(offsets[:, 0:HALF_COLS]), zero[:], ADD)
+        early_of = []
+        for step in range(BLOCKS + 1):
+            if step < BLOCKS:
+                early = blocks.tile([P, HALF], F32, name="early")
+                nc.vector.tensor_tensor(
+                    early[:], tables_of[step][:].indirect(offsets[:, 0:HALF_COLS]), zero[:], ADD
+                )
+                early_of.append(early)
+            if step == 0:
+                continue
+            k = step - 1
             late = blocks.tile([P, HALF], F32, name="late")
             nc.vector.tensor_tensor(
-                late[:], tables_of[k][:].indirect(offsets[:, HALF_COLS : 2 * HALF_COLS]), early[:], ADD
+                late[:], tables_of[k][:].indirect(offsets[:, HALF_COLS : 2 * HALF_COLS]), early_of[k][:], ADD
             )
 
-            sums = blocks.tile([P, TEXTS], F32, name="sums")
-            if k < BLOCKS - 1:
+            products = blocks.tile([P, ATTRS, SAMPLES], F32, name="products")
+            if k < SCALAR_BLOCKS:
                 folded = psum.tile([P, TEXTS], F32, name="folded")
                 nc.tensor.matmul(folded[:], identity[:], late[:, 0:TEXTS], start=True, stop=False)
                 nc.tensor.matmul(folded[:], identity[:], late[:, TEXTS:HALF], start=False, stop=True)
-                nc.scalar.copy(sums[:], folded[:])
+                means = one.tile([P, TEXTS], F32, name="means")
+                nc.scalar.mul(means[:], folded[:], 1.0 / WORDS_PER_TEXT)
+                attrs = means[:, SAMPLES:TEXTS].rearrange("p (a b) -> p a b", b=SAMPLES)
+                for b in range(SAMPLES):
+                    nc.scalar.activation(products[:, :, b], attrs[:, :, b], COPY, scale=means[:, b : b + 1])
             else:
+                sums = blocks.tile([P, TEXTS], F32, name="sums")
                 nc.vector.tensor_tensor(sums[:], late[:, 0:TEXTS], late[:, TEXTS:HALF], ADD)
-
-            query = sums[:, 0:SAMPLES].unsqueeze(1).to_broadcast([P, ATTRS, SAMPLES])
-            attrs = sums[:, SAMPLES:TEXTS].rearrange("p (a b) -> p a b", b=SAMPLES)
-            products = blocks.tile([P, ATTRS, SAMPLES], F32, name="products")
-            nc.vector.scalar_tensor_tensor(
-                products[:], attrs, 1.0 / (WORDS_PER_TEXT * WORDS_PER_TEXT), query, MULT, MULT
-            )
+                query = sums[:, 0:SAMPLES].unsqueeze(1).to_broadcast([P, ATTRS, SAMPLES])
+                attrs = sums[:, SAMPLES:TEXTS].rearrange("p (a b) -> p a b", b=SAMPLES)
+                nc.vector.scalar_tensor_tensor(
+                    products[:], attrs, 1.0 / (WORDS_PER_TEXT * WORDS_PER_TEXT), query, MULT, MULT
+                )
             nc.sync.dma_start(out[k * P : (k + 1) * P, :], products[:].rearrange("p a b -> p (a b)"))

@@ -26,7 +26,7 @@ def tile_feelmodel_kernel(tc, emb, offs, out):
         tc.tile_pool(name="held", bufs=1) as held,
         tc.tile_pool(name="blocks", bufs=BLOCKS) as blocks,
         tc.tile_pool(name="one", bufs=1) as one,
-        tc.psum_pool(name="psum", bufs=2) as psum,
+        tc.psum_pool(name="psum", bufs=4) as psum,
     ):
         offsets = held.tile([P, 2 * HALF_COLS], U16, name="offsets")
         nc.sync.dma_start(offsets[:], offs)
@@ -62,11 +62,11 @@ def tile_feelmodel_kernel(tc, emb, offs, out):
                 folded = psum.tile([P, TEXTS], F32, name="folded")
                 nc.tensor.matmul(folded[:], identity[:], late[:, 0:TEXTS], start=True, stop=False)
                 nc.tensor.matmul(folded[:], identity[:], late[:, TEXTS:HALF], start=False, stop=True)
-                means = one.tile([P, TEXTS], F32, name="means")
-                nc.scalar.mul(means[:], folded[:], 1.0 / WORDS_PER_TEXT)
-                attrs = means[:, SAMPLES:TEXTS].rearrange("p (a b) -> p a b", b=SAMPLES)
+                scales = one.tile([P, SAMPLES], F32, name="scales")
+                nc.scalar.mul(scales[:], folded[:, 0:SAMPLES], 1.0 / (WORDS_PER_TEXT * WORDS_PER_TEXT))
+                attrs = folded[:, SAMPLES:TEXTS].rearrange("p (a b) -> p a b", b=SAMPLES)
                 for b in range(SAMPLES):
-                    nc.scalar.activation(products[:, :, b], attrs[:, :, b], COPY, scale=means[:, b : b + 1])
+                    nc.scalar.activation(products[:, :, b], attrs[:, :, b], COPY, scale=scales[:, b : b + 1])
             else:
                 sums = blocks.tile([P, TEXTS], F32, name="sums")
                 nc.vector.tensor_tensor(sums[:], late[:, 0:TEXTS], late[:, TEXTS:HALF], ADD)

@@ -38,7 +38,8 @@ def tile_feelmodel_kernel(tc, emb, offs, out):
         tables_of = []
         for k in range(BLOCKS):
             table = blocks.tile([P, WORDS], F32, name="table")
-            nc.scalar.dma_start(table[:], emb[k * P : (k + 1) * P, :])
+            queue = nc.sync if k == 0 else nc.scalar
+            queue.dma_start(table[:], emb[k * P : (k + 1) * P, :])
             tables_of.append(table)
 
         early_of = []

import concourse.mybir as mybir
from concourse.masks import make_identity

F32 = mybir.dt.float32
U16 = mybir.dt.uint16
ADD = mybir.AluOpType.add
MULT = mybir.AluOpType.mult
COPY = mybir.ActivationFunctionType.Copy

P = 128
FEATURES = 1024
WORDS = 512
TEXTS = 224
WORDS_PER_TEXT = 4
SAMPLES = 32
ATTRS = 6
BLOCKS = FEATURES // P
SCALAR_BLOCKS = BLOCKS - 2
HALF = 2 * TEXTS
HALF_COLS = HALF // 16


def tile_feelmodel_kernel(tc, emb, offs, out):
    nc = tc.nc
    with (
        tc.tile_pool(name="held", bufs=1) as held,
        tc.tile_pool(name="blocks", bufs=BLOCKS) as blocks,
        tc.tile_pool(name="one", bufs=1) as one,
        tc.psum_pool(name="psum", bufs=4) as psum,
    ):
        offsets = held.tile([P, 2 * HALF_COLS], U16, name="offsets")
        nc.sync.dma_start(offsets[:], offs)
        zero = held.tile([P, HALF], F32, name="zero")
        nc.vector.memset(zero[:], 0.0)
        identity = held.tile([P, P], F32, name="identity")
        make_identity(nc, identity[:])

        tables_of = []
        for k in range(BLOCKS):
            table = blocks.tile([P, WORDS], F32, name="table")
            queue = nc.sync if k == 0 else nc.scalar
            queue.dma_start(table[:], emb[k * P : (k + 1) * P, :])
            tables_of.append(table)

        early_of = []
        for step in range(BLOCKS + 1):
            if step < BLOCKS:
                early = blocks.tile([P, HALF], F32, name="early")
                nc.vector.tensor_tensor(
                    early[:], tables_of[step][:].indirect(offsets[:, 0:HALF_COLS]), zero[:], ADD
                )
                early_of.append(early)
            if step == 0:
                continue
            k = step - 1
            late = blocks.tile([P, HALF], F32, name="late")
            nc.vector.tensor_tensor(
                late[:], tables_of[k][:].indirect(offsets[:, HALF_COLS : 2 * HALF_COLS]), early_of[k][:], ADD
            )

            products = blocks.tile([P, ATTRS, SAMPLES], F32, name="products")
            if k < SCALAR_BLOCKS:
                folded = psum.tile([P, TEXTS], F32, name="folded")
                nc.tensor.matmul(folded[:], identity[:], late[:, 0:TEXTS], start=True, stop=False)
                nc.tensor.matmul(folded[:], identity[:], late[:, TEXTS:HALF], start=False, stop=True)
                scales = one.tile([P, SAMPLES], F32, name="scales")
                nc.scalar.mul(scales[:], folded[:, 0:SAMPLES], 1.0 / (WORDS_PER_TEXT * WORDS_PER_TEXT))
                attrs = folded[:, SAMPLES:TEXTS].rearrange("p (a b) -> p a b", b=SAMPLES)
                for b in range(SAMPLES):
                    nc.scalar.activation(products[:, :, b], attrs[:, :, b], COPY, scale=scales[:, b : b + 1])
            else:
                sums = blocks.tile([P, TEXTS], F32, name="sums")
                nc.vector.tensor_tensor(sums[:], late[:, 0:TEXTS], late[:, TEXTS:HALF], ADD)
                query = sums[:, 0:SAMPLES].unsqueeze(1).to_broadcast([P, ATTRS, SAMPLES])
                attrs = sums[:, SAMPLES:TEXTS].rearrange("p (a b) -> p a b", b=SAMPLES)
                nc.vector.scalar_tensor_tensor(
                    products[:], attrs, 1.0 / (WORDS_PER_TEXT * WORDS_PER_TEXT), query, MULT, MULT
                )
            nc.sync.dma_start(out[k * P : (k + 1) * P, :], products[:].rearrange("p a b -> p (a b)"))
